import numpy as np
import ml_dtypes


def mxq(x, axis, fmt="e4m3"):
    dtype, down = {"e4m3": (ml_dtypes.float8_e4m3fn, 7), "e5m2": (ml_dtypes.float8_e5m2, 14)}[fmt]
    v = np.moveaxis(np.asarray(x, np.float32).astype(ml_dtypes.bfloat16).astype(np.float64), axis, -1)
    blocks = v.reshape(v.shape[:-1] + (-1, 32))
    amax = np.abs(blocks).max(-1, keepdims=True)
    byte = np.maximum(np.where(amax > 0, np.frexp(amax)[1] - 1 + 127, 0) - down, 1)
    scale = np.exp2(byte - 127.0)
    codes = (blocks / scale).astype(np.float32).astype(dtype).astype(np.float64)
    return np.moveaxis((codes * scale).reshape(v.shape), -1, axis)


WIDE = False


def mx_kscale(k):
    if not WIDE:
        return np.ones(k)
    levels = np.array([10, -10, 5, -5, 0])
    a = np.random.permutation(np.resize(levels, k // 512 * 4)).reshape(k // 512, 4)
    idx = np.arange(k)
    return np.exp2(a[idx // 512, idx % 128 // 32])


BF16 = ml_dtypes.bfloat16


def bf(x):
    return np.asarray(x, np.float32).astype(BF16)


def f64(x):
    return np.asarray(x).astype(np.float64)


N, NFEAT, NHEADS, NHID, NCLASS = 1024, 512, 4, 128, 128
P = 0.08


def elu(v):
    return np.where(v > 0, v, np.exp(np.minimum(v, 0.0)) - 1.0)


def setup_inputs():
    s, t = mx_kscale(NFEAT), mx_kscale(N)
    edges = np.random.random((N, N)) < P
    return {"x": bf(np.random.standard_normal((N, NFEAT)) * s / t[:, None]),
            "adj": bf(edges * (0.5 + np.random.random((N, N))) * t),
            "W0": bf(np.random.standard_normal((NHEADS, NFEAT, NHID)) * 1.5 / np.sqrt(NFEAT * P * N) / s[:, None])}


def reference(x, adj, W0):
    h = mxq(f64(x), 1, "e4m3") @ mxq(f64(W0), 1, "e4m3")
    hp = mxq(f64(adj), 1, "e4m3") @ mxq(h, 1, "e4m3")
    return elu(hp).transpose(1, 0, 2).reshape(N, NHEADS * NHID)

@@ -1,0 +1,187 @@
+from contextlib import ExitStack
+
+import concourse.mybir as mybir
+from concourse.masks import make_identity
+
+F32 = mybir.dt.float32
+BF16 = mybir.dt.bfloat16
+U32 = mybir.dt.uint32
+U8 = mybir.dt.uint8
+FP8X4 = mybir.dt.float8_e4m3fn_x4
+ALU = mybir.AluOpType
+ACT = mybir.ActivationFunctionType
+
+P = 128
+PACK = 4
+K_PASS = P * PACK
+NODES = 1024
+FEATS = 512
+HEADS = 4
+HIDDEN = 128
+WIDTH = HEADS * HIDDEN
+NODE_PASSES = NODES // K_PASS
+ROW_TILES = NODES // P
+ROWS_PER_LOAD = 2
+LOOKAHEAD = 3
+
+FLOPS = 2 * NODES * FEATS * WIDTH + 2 * NODES * NODES * WIDTH
+
+
+def tile_gat_pa_kernel(tc, x, adj, W0, out):
+    nc = tc.nc
+    with ExitStack() as ctx:
+        keep = ctx.enter_context(tc.tile_pool(name="keep", bufs=1))
+        banks = ctx.enter_context(tc.psum_pool(name="banks", bufs=8))
+
+        w_sb = keep.tile([P, HEADS, PACK, HIDDEN], BF16, name="w_sb")
+        x_sb = []
+        for c in range(NODE_PASSES):
+            x_rows = keep.tile([P, PACK, FEATS], BF16, name="x_sb%d" % c)
+            nc.sync.dma_start(
+                out=x_rows[:].rearrange("p (u e) k -> p u (e k)", u=2),
+                in_=x[c * K_PASS : (c + 1) * K_PASS, :].rearrange("(u p e) k -> p u (e k)", u=2, e=2),
+            )
+            x_sb.append(x_rows)
+            if c == 0:
+                for h in range(HEADS):
+                    nc.sync.dma_start(
+                        out=w_sb[:, h].rearrange("p (u e) f -> p u (e f)", u=2),
+                        in_=W0[h].rearrange("(u p e) f -> p u (e f)", u=2, e=2),
+                    )
+        adj_rows = adj.rearrange("(p i) m -> p i m", i=ROW_TILES)
+        adj_sb = []
+        for j in range(ROW_TILES // ROWS_PER_LOAD):
+            a_rows = keep.tile([P, ROWS_PER_LOAD, NODES], BF16, name="adj_sb%d" % j)
+            nc.sync.dma_start(out=a_rows[:], in_=adj_rows[:, j * ROWS_PER_LOAD : (j + 1) * ROWS_PER_LOAD, :])
+            adj_sb.append(a_rows)
+
+        ident = keep.tile([P, P], F32, name="ident")
+        make_identity(nc, ident[:])
+
+        warm = keep.tile([P, 1], F32, name="warm")
+        nc.vector.memset(warm[:], 0.0)
+        nc.scalar.activation(out=warm[:], in_=warm[:], func=ACT.Exp)
+
+        w_grp = keep.tile([P, WIDTH, PACK], BF16, name="w_grp", align_bytes=64)
+        w_codes = keep.tile([P, WIDTH], U32, name="w_codes", align_bytes=64)
+        w_scales = keep.tile([P, WIDTH], U8, name="w_scales", align_bytes=64)
+        for h in range(HEADS):
+            cols = slice(h * HIDDEN, (h + 1) * HIDDEN)
+            dst = w_grp[:, cols, :].rearrange("p (c i) t -> p c t i", i=4)
+            src = w_sb[:, h].rearrange("p t (c i) -> p c t i", i=4)
+            if h >= HEADS // 2:
+                nc.scalar.copy(out=dst, in_=src)
+            else:
+                nc.vector.tensor_copy(out=dst, in_=src)
+        for h in range(HEADS):
+            cols = slice(h * HIDDEN, (h + 1) * HIDDEN)
+            nc.vector.quantize_mx(
+                out=w_codes[:, cols].bitcast(FP8X4),
+                scales=w_scales[:, cols],
+                in_=w_grp[:, cols, :].rearrange("p f t -> p (f t)"),
+            )
+
+        x_codes = []
+        x_scales = []
+        for c in range(NODE_PASSES):
+            x_words = x_sb[c][:].bitcast(F32)
+            x_grp = keep.tile([P, PACK, P, PACK], BF16, name="x_grp%d" % c, align_bytes=64)
+            for b in range(2):
+                xT = banks.tile([P, 2, 2, P], F32, tag="bank", name="xT")
+                for tl in range(2):
+                    for u in range(2):
+                        nc.tensor.transpose(xT[:, tl, u, :], x_words[:, 2 * b + tl, u * P : (u + 1) * P], ident[:])
+                dst = x_grp[:].bitcast(F32)[:, 2 * b : 2 * b + 2, :, :]
+                src = xT[:].rearrange("p t u n -> p t n u")
+                if b == 0:
+                    nc.scalar.copy(out=dst, in_=src)
+                else:
+                    nc.vector.tensor_copy(out=dst, in_=src)
+            codes = keep.tile([P, K_PASS], U32, name="x_codes%d" % c, align_bytes=64)
+            scales = keep.tile([P, K_PASS], U8, name="x_scales%d" % c, align_bytes=64)
+            nc.vector.quantize_mx(
+                out=codes[:].bitcast(FP8X4),
+                scales=scales[:],
+                in_=x_grp[:].rearrange("p t n j -> p (t n j)"),
+            )
+            x_codes.append(codes)
+            x_scales.append(scales)
+
+        g_codes = []
+        g_scales = []
+        for c in range(NODE_PASSES):
+            g_grp = keep.tile([P, WIDTH, PACK], BF16, name="g_grp%d" % c, align_bytes=64)
+            for h in range(HEADS):
+                cols = slice(h * HIDDEN, (h + 1) * HIDDEN)
+                g_ps = banks.tile([P, PACK, HIDDEN], F32, tag="bank", name="g_ps")
+                for t in range(PACK):
+                    nodes = slice(t * P, (t + 1) * P)
+                    nc.tensor.matmul_mx(
+                        out=g_ps[:, t, :],
+                        lhsT=x_codes[c][:, nodes].bitcast(FP8X4),
+                        lhsT_scale=x_scales[c][:, nodes],
+                        rhs=w_codes[:, cols].bitcast(FP8X4),
+                        rhs_scale=w_scales[:, cols],
+                        start=True,
+                        stop=True,
+                    )
+                dst = g_grp[:, cols, :]
+                src = g_ps[:].rearrange("p t f -> p f t")
+                if h % 2 == 0:
+                    nc.vector.tensor_copy(out=dst, in_=src)
+                else:
+                    nc.scalar.copy(out=dst, in_=src)
+            codes = keep.tile([P, WIDTH], U32, name="g_codes%d" % c, align_bytes=64)
+            scales = keep.tile([P, WIDTH], U8, name="g_scales%d" % c, align_bytes=64)
+            nc.vector.quantize_mx(
+                out=codes[:].bitcast(FP8X4),
+                scales=scales[:],
+                in_=g_grp[:].rearrange("p f t -> p (f t)"),
+            )
+            g_codes.append(codes)
+            g_scales.append(scales)
+
+        a_codes = []
+        a_scales = []
+
+        def prepare_adj(i):
+            a_words = adj_sb[i // ROWS_PER_LOAD][:].bitcast(F32)
+            aT = banks.tile([P, PACK, P], F32, tag="bank", name="aT")
+            for s in range(PACK):
+                nc.tensor.transpose(aT[:, s, :], a_words[:, i % ROWS_PER_LOAD, s * P : (s + 1) * P], ident[:])
+            a_grp = keep.tile([P, NODE_PASSES, P, PACK], BF16, name="a_grp%d" % i, align_bytes=64)
+            nc.scalar.copy(out=a_grp[:].bitcast(F32), in_=aT[:].rearrange("p (c u) n -> p c n u", u=2))
+            codes = keep.tile([P, NODE_PASSES * P], U32, name="a_codes%d" % i, align_bytes=64)
+            scales = keep.tile([P, NODE_PASSES * P], U8, name="a_scales%d" % i, align_bytes=64)
+            nc.vector.quantize_mx(
+                out=codes[:].bitcast(FP8X4),
+                scales=scales[:],
+                in_=a_grp[:].rearrange("p c n j -> p (c n j)"),
+            )
+            a_codes.append(codes)
+            a_scales.append(scales)
+
+        out_rows = out.rearrange("(p i) d -> p i d", i=ROW_TILES)
+        for i in range(LOOKAHEAD):
+            prepare_adj(i)
+        for i in range(ROW_TILES):
+            p_ps = banks.tile([P, WIDTH], F32, tag="bank", name="p_ps")
+            for c in range(NODE_PASSES):
+                rows = slice(c * P, (c + 1) * P)
+                nc.tensor.matmul_mx(
+                    out=p_ps[:],
+                    lhsT=a_codes[i][:, rows].bitcast(FP8X4),
+                    lhsT_scale=a_scales[i][:, rows],
+                    rhs=g_codes[c][:].bitcast(FP8X4),
+                    rhs_scale=g_scales[c][:],
+                    start=(c == 0),
+                    stop=(c == NODE_PASSES - 1),
+                )
+            neg = keep.tile([P, WIDTH], F32, name="neg%d" % i)
+            nc.scalar.activation(out=neg[:], in_=p_ps[:], func=ACT.Exp)
+            nc.vector.tensor_scalar(out=neg[:], in0=neg[:], scalar1=-1.0, scalar2=0.0, op0=ALU.add, op1=ALU.min)
+            res = keep.tile([P, WIDTH], F32, name="res%d" % i)
+            nc.vector.tensor_tensor(out=res[:], in0=p_ps[:], in1=neg[:], op=ALU.max)
+            nc.sync.dma_start(out=out_rows[:, i, :], in_=res[:])
+            if i + LOOKAHEAD < ROW_TILES:
+                prepare_adj(i + LOOKAHEAD)

@@ -22,6 +22,8 @@ WIDTH = HEADS * HIDDEN
 NODE_PASSES = NODES // K_PASS
 ROW_TILES = NODES // P
 ROWS_PER_LOAD = 2
+WARM_BEFORE = 5
+WARM_AFTER = 3
 LOOKAHEAD = 3
 
 FLOPS = 2 * NODES * FEATS * WIDTH + 2 * NODES * NODES * WIDTH
@@ -62,6 +64,12 @@ def tile_gat_pa_kernel(tc, x, adj, W0, out):
         nc.vector.memset(warm[:], 0.0)
         nc.scalar.activation(out=warm[:], in_=warm[:], func=ACT.Exp)
 
+        idle_in = keep.tile([P, WIDTH], BF16, name="idle_in")
+        nc.vector.memset(idle_in[:], 0.0)
+        idle_ps = banks.tile([P, WIDTH], F32, tag="bank", name="idle_ps")
+        for r in range(WARM_BEFORE):
+            nc.tensor.matmul(out=idle_ps[:], lhsT=idle_in[:, 0:P], rhs=idle_in[:], start=True, stop=True)
+
         w_grp = keep.tile([P, WIDTH, PACK], BF16, name="w_grp", align_bytes=64)
         w_codes = keep.tile([P, WIDTH], U32, name="w_codes", align_bytes=64)
         w_scales = keep.tile([P, WIDTH], U8, name="w_scales", align_bytes=64)
@@ -97,6 +105,9 @@ def tile_gat_pa_kernel(tc, x, adj, W0, out):
                     nc.scalar.copy(out=dst, in_=src)
                 else:
                     nc.vector.tensor_copy(out=dst, in_=src)
+            if c == 0:
+                for r in range(WARM_AFTER):
+                    nc.tensor.matmul(out=idle_ps[:], lhsT=x_sb[0][:, 0, 0:P], rhs=x_sb[0][:, 1, :], start=True, stop=True)
             codes = keep.tile([P, K_PASS], U32, name="x_codes%d" % c, align_bytes=64)
             scales = keep.tile([P, K_PASS], U8, name="x_scales%d" % c, align_bytes=64)
             nc.vector.quantize_mx(

@@ -22,9 +22,7 @@ WIDTH = HEADS * HIDDEN
 NODE_PASSES = NODES // K_PASS
 ROW_TILES = NODES // P
 ROWS_PER_LOAD = 2
-WARM_BEFORE = 5
-WARM_AFTER = 3
-LOOKAHEAD = 3
+LOOKAHEAD = 4
 
 FLOPS = 2 * NODES * FEATS * WIDTH + 2 * NODES * NODES * WIDTH
 
@@ -35,8 +33,14 @@ def tile_gat_pa_kernel(tc, x, adj, W0, out):
         keep = ctx.enter_context(tc.tile_pool(name="keep", bufs=1))
         banks = ctx.enter_context(tc.psum_pool(name="banks", bufs=8))
 
-        w_sb = keep.tile([P, HEADS, PACK, HIDDEN], BF16, name="w_sb")
+        def quantise(name, grouped, width):
+            codes = keep.tile([P, width], U32, name=name + "_codes", align_bytes=64)
+            scales = keep.tile([P, width], U8, name=name + "_scales", align_bytes=64)
+            nc.vector.quantize_mx(out=codes[:].bitcast(FP8X4), scales=scales[:], in_=grouped)
+            return codes, scales
+
         x_sb = []
+        w_sb = []
         for c in range(NODE_PASSES):
             x_rows = keep.tile([P, PACK, FEATS], BF16, name="x_sb%d" % c)
             nc.sync.dma_start(
@@ -46,10 +50,12 @@ def tile_gat_pa_kernel(tc, x, adj, W0, out):
             x_sb.append(x_rows)
             if c == 0:
                 for h in range(HEADS):
+                    w_rows = keep.tile([P, PACK, HIDDEN], BF16, name="w_sb%d" % h)
                     nc.sync.dma_start(
-                        out=w_sb[:, h].rearrange("p (u e) f -> p u (e f)", u=2),
+                        out=w_rows[:].rearrange("p (u e) f -> p u (e f)", u=2),
                         in_=W0[h].rearrange("(u p e) f -> p u (e f)", u=2, e=2),
                     )
+                    w_sb.append(w_rows)
         adj_rows = adj.rearrange("(p i) m -> p i m", i=ROW_TILES)
         adj_sb = []
         for j in range(ROW_TILES // ROWS_PER_LOAD):
@@ -64,135 +70,115 @@ def tile_gat_pa_kernel(tc, x, adj, W0, out):
         nc.vector.memset(warm[:], 0.0)
         nc.scalar.activation(out=warm[:], in_=warm[:], func=ACT.Exp)
 
-        idle_in = keep.tile([P, WIDTH], BF16, name="idle_in")
-        nc.vector.memset(idle_in[:], 0.0)
-        idle_ps = banks.tile([P, WIDTH], F32, tag="bank", name="idle_ps")
-        for r in range(WARM_BEFORE):
-            nc.tensor.matmul(out=idle_ps[:], lhsT=idle_in[:, 0:P], rhs=idle_in[:], start=True, stop=True)
-
-        w_grp = keep.tile([P, WIDTH, PACK], BF16, name="w_grp", align_bytes=64)
-        w_codes = keep.tile([P, WIDTH], U32, name="w_codes", align_bytes=64)
-        w_scales = keep.tile([P, WIDTH], U8, name="w_scales", align_bytes=64)
-        for h in range(HEADS):
-            cols = slice(h * HIDDEN, (h + 1) * HIDDEN)
-            dst = w_grp[:, cols, :].rearrange("p (c i) t -> p c t i", i=4)
-            src = w_sb[:, h].rearrange("p t (c i) -> p c t i", i=4)
-            if h >= HEADS // 2:
-                nc.scalar.copy(out=dst, in_=src)
-            else:
-                nc.vector.tensor_copy(out=dst, in_=src)
-        for h in range(HEADS):
-            cols = slice(h * HIDDEN, (h + 1) * HIDDEN)
-            nc.vector.quantize_mx(
-                out=w_codes[:, cols].bitcast(FP8X4),
-                scales=w_scales[:, cols],
-                in_=w_grp[:, cols, :].rearrange("p f t -> p (f t)"),
-            )
-
-        x_codes = []
-        x_scales = []
-        for c in range(NODE_PASSES):
+        def transpose_x(c):
             x_words = x_sb[c][:].bitcast(F32)
-            x_grp = keep.tile([P, PACK, P, PACK], BF16, name="x_grp%d" % c, align_bytes=64)
+            grouped = []
             for b in range(2):
                 xT = banks.tile([P, 2, 2, P], F32, tag="bank", name="xT")
                 for tl in range(2):
                     for u in range(2):
                         nc.tensor.transpose(xT[:, tl, u, :], x_words[:, 2 * b + tl, u * P : (u + 1) * P], ident[:])
-                dst = x_grp[:].bitcast(F32)[:, 2 * b : 2 * b + 2, :, :]
-                src = xT[:].rearrange("p t u n -> p t n u")
-                if b == 0:
-                    nc.scalar.copy(out=dst, in_=src)
-                else:
-                    nc.vector.tensor_copy(out=dst, in_=src)
-            if c == 0:
-                for r in range(WARM_AFTER):
-                    nc.tensor.matmul(out=idle_ps[:], lhsT=x_sb[0][:, 0, 0:P], rhs=x_sb[0][:, 1, :], start=True, stop=True)
-            codes = keep.tile([P, K_PASS], U32, name="x_codes%d" % c, align_bytes=64)
-            scales = keep.tile([P, K_PASS], U8, name="x_scales%d" % c, align_bytes=64)
-            nc.vector.quantize_mx(
-                out=codes[:].bitcast(FP8X4),
-                scales=scales[:],
-                in_=x_grp[:].rearrange("p t n j -> p (t n j)"),
-            )
-            x_codes.append(codes)
-            x_scales.append(scales)
+                x_grp = keep.tile([P, 2, P, PACK], BF16, name="x_grp%d%d" % (c, b), align_bytes=64)
+                nc.scalar.copy(out=x_grp[:].bitcast(F32), in_=xT[:].rearrange("p t u n -> p t n u"))
+                grouped.append(x_grp)
+            return grouped
 
-        g_codes = []
-        g_scales = []
-        for c in range(NODE_PASSES):
-            g_grp = keep.tile([P, WIDTH, PACK], BF16, name="g_grp%d" % c, align_bytes=64)
-            for h in range(HEADS):
-                cols = slice(h * HIDDEN, (h + 1) * HIDDEN)
-                g_ps = banks.tile([P, PACK, HIDDEN], F32, tag="bank", name="g_ps")
-                for t in range(PACK):
-                    nodes = slice(t * P, (t + 1) * P)
-                    nc.tensor.matmul_mx(
-                        out=g_ps[:, t, :],
-                        lhsT=x_codes[c][:, nodes].bitcast(FP8X4),
-                        lhsT_scale=x_scales[c][:, nodes],
-                        rhs=w_codes[:, cols].bitcast(FP8X4),
-                        rhs_scale=w_scales[:, cols],
-                        start=True,
-                        stop=True,
-                    )
-                dst = g_grp[:, cols, :]
-                src = g_ps[:].rearrange("p t f -> p f t")
-                if h % 2 == 0:
-                    nc.vector.tensor_copy(out=dst, in_=src)
-                else:
-                    nc.scalar.copy(out=dst, in_=src)
-            codes = keep.tile([P, WIDTH], U32, name="g_codes%d" % c, align_bytes=64)
-            scales = keep.tile([P, WIDTH], U8, name="g_scales%d" % c, align_bytes=64)
-            nc.vector.quantize_mx(
-                out=codes[:].bitcast(FP8X4),
-                scales=scales[:],
-                in_=g_grp[:].rearrange("p f t -> p (f t)"),
-            )
-            g_codes.append(codes)
-            g_scales.append(scales)
+        def quantise_x(c, grouped):
+            return [
+                quantise("x%d%d" % (c, b), grouped[b][:].rearrange("p t n j -> p (t n j)"), 2 * P) for b in range(2)
+            ]
 
-        a_codes = []
-        a_scales = []
-
-        def prepare_adj(i):
+        def transpose_adj(i):
             a_words = adj_sb[i // ROWS_PER_LOAD][:].bitcast(F32)
             aT = banks.tile([P, PACK, P], F32, tag="bank", name="aT")
             for s in range(PACK):
                 nc.tensor.transpose(aT[:, s, :], a_words[:, i % ROWS_PER_LOAD, s * P : (s + 1) * P], ident[:])
             a_grp = keep.tile([P, NODE_PASSES, P, PACK], BF16, name="a_grp%d" % i, align_bytes=64)
             nc.scalar.copy(out=a_grp[:].bitcast(F32), in_=aT[:].rearrange("p (c u) n -> p c n u", u=2))
-            codes = keep.tile([P, NODE_PASSES * P], U32, name="a_codes%d" % i, align_bytes=64)
-            scales = keep.tile([P, NODE_PASSES * P], U8, name="a_scales%d" % i, align_bytes=64)
-            nc.vector.quantize_mx(
-                out=codes[:].bitcast(FP8X4),
-                scales=scales[:],
-                in_=a_grp[:].rearrange("p c n j -> p (c n j)"),
+            return a_grp
+
+        def quantise_adj(i, a_grp):
+            return quantise("a%d" % i, a_grp[:].rearrange("p c n j -> p (c n j)"), NODE_PASSES * P)
+
+        w_grp = []
+        for h in range(HEADS):
+            grouped = keep.tile([P, HIDDEN, PACK], BF16, name="w_grp%d" % h, align_bytes=64)
+            nc.vector.tensor_copy(
+                out=grouped[:].rearrange("p (c i) t -> p c t i", i=4),
+                in_=w_sb[h][:].rearrange("p t (c i) -> p c t i", i=4),
             )
-            a_codes.append(codes)
-            a_scales.append(scales)
+            w_grp.append(grouped)
+        x_grp0 = transpose_x(0)
+        x_q = [quantise_x(0, x_grp0)]
+        w_q = [quantise("w%d" % h, w_grp[h][:].rearrange("p f t -> p (f t)"), HIDDEN) for h in range(HEADS)]
+        x_grp1 = transpose_x(1)
+        x_q.append(quantise_x(1, x_grp1))
+
+        a_q = []
+        g_q = []
+        for c in range(NODE_PASSES):
+            g_codes = keep.tile([P, WIDTH], U32, name="g_codes%d" % c, align_bytes=64)
+            g_scales = keep.tile([P, WIDTH], U8, name="g_scales%d" % c, align_bytes=64)
+            g_grp = []
+
+            def quantise_g(h):
+                cols = slice(h * HIDDEN, (h + 1) * HIDDEN)
+                nc.vector.quantize_mx(
+                    out=g_codes[:, cols].bitcast(FP8X4),
+                    scales=g_scales[:, cols],
+                    in_=g_grp[h][:].rearrange("p f t -> p (f t)"),
+                )
+
+            for h in range(HEADS):
+                g_ps = banks.tile([P, PACK, HIDDEN], F32, tag="bank", name="g_ps")
+                for t in range(PACK):
+                    x_codes, x_scales = x_q[c][t // 2]
+                    nodes = slice((t % 2) * P, (t % 2 + 1) * P)
+                    nc.tensor.matmul_mx(
+                        out=g_ps[:, t, :],
+                        lhsT=x_codes[:, nodes].bitcast(FP8X4),
+                        lhsT_scale=x_scales[:, nodes],
+                        rhs=w_q[h][0][:].bitcast(FP8X4),
+                        rhs_scale=w_q[h][1][:],
+                        start=True,
+                        stop=True,
+                    )
+                grouped = keep.tile([P, HIDDEN, PACK], BF16, name="g_grp%d%d" % (c, h), align_bytes=64)
+                if h % 2 == 0:
+                    nc.scalar.copy(out=grouped[:], in_=g_ps[:].rearrange("p t f -> p f t"))
+                else:
+                    nc.vector.tensor_copy(out=grouped[:], in_=g_ps[:].rearrange("p t f -> p f t"))
+                g_grp.append(grouped)
+                if h > 0:
+                    quantise_g(h - 1)
+            a_grp = transpose_adj(c)
+            quantise_g(HEADS - 1)
+            g_q.append((g_codes, g_scales))
+            a_q.append(quantise_adj(c, a_grp))
+        for i in range(NODE_PASSES, LOOKAHEAD):
+            a_q.append(quantise_adj(i, transpose_adj(i)))
 
         out_rows = out.rearrange("(p i) d -> p i d", i=ROW_TILES)
-        for i in range(LOOKAHEAD):
-            prepare_adj(i)
         for i in range(ROW_TILES):
             p_ps = banks.tile([P, WIDTH], F32, tag="bank", name="p_ps")
             for c in range(NODE_PASSES):
                 rows = slice(c * P, (c + 1) * P)
                 nc.tensor.matmul_mx(
                     out=p_ps[:],
-                    lhsT=a_codes[i][:, rows].bitcast(FP8X4),
-                    lhsT_scale=a_scales[i][:, rows],
-                    rhs=g_codes[c][:].bitcast(FP8X4),
-                    rhs_scale=g_scales[c][:],
+                    lhsT=a_q[i][0][:, rows].bitcast(FP8X4),
+                    lhsT_scale=a_q[i][1][:, rows],
+                    rhs=g_q[c][0][:].bitcast(FP8X4),
+                    rhs_scale=g_q[c][1][:],
                     start=(c == 0),
                     stop=(c == NODE_PASSES - 1),
                 )
             neg = keep.tile([P, WIDTH], F32, name="neg%d" % i)
             nc.scalar.activation(out=neg[:], in_=p_ps[:], func=ACT.Exp)
+            if i + LOOKAHEAD < ROW_TILES:
+                a_grp = transpose_adj(i + LOOKAHEAD)
             nc.vector.tensor_scalar(out=neg[:], in0=neg[:], scalar1=-1.0, scalar2=0.0, op0=ALU.add, op1=ALU.min)
             res = keep.tile([P, WIDTH], F32, name="res%d" % i)
             nc.vector.tensor_tensor(out=res[:], in0=p_ps[:], in1=neg[:], op=ALU.max)
             nc.sync.dma_start(out=out_rows[:, i, :], in_=res[:])
             if i + LOOKAHEAD < ROW_TILES:
-                prepare_adj(i + LOOKAHEAD)
+                a_q.append(quantise_adj(i + LOOKAHEAD, a_grp))

@@ -32,6 +32,7 @@ def tile_gat_pa_kernel(tc, x, adj, W0, out):
     with ExitStack() as ctx:
         keep = ctx.enter_context(tc.tile_pool(name="keep", bufs=1))
         banks = ctx.enter_context(tc.psum_pool(name="banks", bufs=8))
+        ctx.enter_context(tc.manual_schedule())
 
         def quantise(name, grouped, width):
             codes = keep.tile([P, width], U32, name=name + "_codes", align_bytes=64)

@@ -32,7 +32,6 @@ def tile_gat_pa_kernel(tc, x, adj, W0, out):
     with ExitStack() as ctx:
         keep = ctx.enter_context(tc.tile_pool(name="keep", bufs=1))
         banks = ctx.enter_context(tc.psum_pool(name="banks", bufs=8))
-        ctx.enter_context(tc.manual_schedule())
 
         def quantise(name, grouped, width):
             codes = keep.tile([P, width], U32, name=name + "_codes", align_bytes=64)
@@ -177,9 +176,9 @@ def tile_gat_pa_kernel(tc, x, adj, W0, out):
             nc.scalar.activation(out=neg[:], in_=p_ps[:], func=ACT.Exp)
             if i + LOOKAHEAD < ROW_TILES:
                 a_grp = transpose_adj(i + LOOKAHEAD)
-            nc.vector.tensor_scalar(out=neg[:], in0=neg[:], scalar1=-1.0, scalar2=0.0, op0=ALU.add, op1=ALU.min)
+            nc.gpsimd.tensor_scalar(out=neg[:], in0=neg[:], scalar1=1.0, scalar2=0.0, op0=ALU.min, op1=ALU.max)
             res = keep.tile([P, WIDTH], F32, name="res%d" % i)
-            nc.vector.tensor_tensor(out=res[:], in0=p_ps[:], in1=neg[:], op=ALU.max)
+            nc.vector.scalar_tensor_tensor(out=res[:], in0=neg[:], scalar=-1.0, in1=p_ps[:], op0=ALU.add, op1=ALU.max)
             nc.sync.dma_start(out=out_rows[:, i, :], in_=res[:])
             if i + LOOKAHEAD < ROW_TILES:
                 a_q.append(quantise_adj(i + LOOKAHEAD, a_grp))

@@ -22,6 +22,7 @@ WIDTH = HEADS * HIDDEN
 NODE_PASSES = NODES // K_PASS
 ROW_TILES = NODES // P
 ROWS_PER_LOAD = 2
+CLAMPS_ON_GPSIMD = 6
 LOOKAHEAD = 4
 
 FLOPS = 2 * NODES * FEATS * WIDTH + 2 * NODES * NODES * WIDTH
@@ -70,96 +71,125 @@ def tile_gat_pa_kernel(tc, x, adj, W0, out):
         nc.vector.memset(warm[:], 0.0)
         nc.scalar.activation(out=warm[:], in_=warm[:], func=ACT.Exp)
 
-        def transpose_x(c):
+        def transpose_x(c, b):
             x_words = x_sb[c][:].bitcast(F32)
-            grouped = []
-            for b in range(2):
-                xT = banks.tile([P, 2, 2, P], F32, tag="bank", name="xT")
-                for tl in range(2):
-                    for u in range(2):
-                        nc.tensor.transpose(xT[:, tl, u, :], x_words[:, 2 * b + tl, u * P : (u + 1) * P], ident[:])
-                x_grp = keep.tile([P, 2, P, PACK], BF16, name="x_grp%d%d" % (c, b), align_bytes=64)
-                nc.scalar.copy(out=x_grp[:].bitcast(F32), in_=xT[:].rearrange("p t u n -> p t n u"))
-                grouped.append(x_grp)
+            xT = banks.tile([P, 2, 2, P], F32, tag="bank", name="xT")
+            for tl in range(2):
+                for u in range(2):
+                    nc.tensor.transpose(xT[:, tl, u, :], x_words[:, 2 * b + tl, u * P : (u + 1) * P], ident[:])
+            return xT
+
+        def group_x(c, b, xT):
+            x_grp = keep.tile([P, 2, P, PACK], BF16, name="x_grp%d%d" % (c, b), align_bytes=64)
+            nc.scalar.copy(out=x_grp[:].bitcast(F32), in_=xT[:].rearrange("p t u n -> p t n u"))
+            return x_grp
+
+        def quantise_x(c, b, x_grp):
+            return quantise("x%d%d" % (c, b), x_grp[:].rearrange("p t n j -> p (t n j)"), 2 * P)
+
+        def group_w(h):
+            grouped = keep.tile([P, HIDDEN, PACK], BF16, name="w_grp%d" % h, align_bytes=64)
+            nc.vector.tensor_copy(
+                out=grouped[:].rearrange("p (c i) t -> p c t i", i=4),
+                in_=w_sb[h][:].rearrange("p t (c i) -> p c t i", i=4),
+            )
             return grouped
 
-        def quantise_x(c, grouped):
-            return [
-                quantise("x%d%d" % (c, b), grouped[b][:].rearrange("p t n j -> p (t n j)"), 2 * P) for b in range(2)
-            ]
+        def quantise_w(h, grouped):
+            return quantise("w%d" % h, grouped[:].rearrange("p f t -> p (f t)"), HIDDEN)
 
         def transpose_adj(i):
             a_words = adj_sb[i // ROWS_PER_LOAD][:].bitcast(F32)
             aT = banks.tile([P, PACK, P], F32, tag="bank", name="aT")
             for s in range(PACK):
                 nc.tensor.transpose(aT[:, s, :], a_words[:, i % ROWS_PER_LOAD, s * P : (s + 1) * P], ident[:])
+            return aT
+
+        def group_adj(i, aT):
             a_grp = keep.tile([P, NODE_PASSES, P, PACK], BF16, name="a_grp%d" % i, align_bytes=64)
-            nc.scalar.copy(out=a_grp[:].bitcast(F32), in_=aT[:].rearrange("p (c u) n -> p c n u", u=2))
+            out, in_ = a_grp[:].bitcast(F32), aT[:].rearrange("p (c u) n -> p c n u", u=2)
+            if i % 3 == 2:
+                nc.vector.tensor_copy(out=out, in_=in_)
+            else:
+                nc.scalar.copy(out=out, in_=in_)
             return a_grp
 
         def quantise_adj(i, a_grp):
             return quantise("a%d" % i, a_grp[:].rearrange("p c n j -> p (c n j)"), NODE_PASSES * P)
 
-        w_grp = []
-        for h in range(HEADS):
-            grouped = keep.tile([P, HIDDEN, PACK], BF16, name="w_grp%d" % h, align_bytes=64)
-            nc.vector.tensor_copy(
-                out=grouped[:].rearrange("p (c i) t -> p c t i", i=4),
-                in_=w_sb[h][:].rearrange("p t (c i) -> p c t i", i=4),
-            )
-            w_grp.append(grouped)
-        x_grp0 = transpose_x(0)
-        x_q = [quantise_x(0, x_grp0)]
-        w_q = [quantise("w%d" % h, w_grp[h][:].rearrange("p f t -> p (f t)"), HIDDEN) for h in range(HEADS)]
-        x_grp1 = transpose_x(1)
-        x_q.append(quantise_x(1, x_grp1))
+        def multiply_g(c, h):
+            g_ps = banks.tile([P, PACK, HIDDEN], F32, tag="bank", name="g_ps")
+            for t in range(PACK):
+                x_codes, x_scales = x_q[c][t // 2]
+                nodes = slice((t % 2) * P, (t % 2 + 1) * P)
+                nc.tensor.matmul_mx(
+                    out=g_ps[:, t, :],
+                    lhsT=x_codes[:, nodes].bitcast(FP8X4),
+                    lhsT_scale=x_scales[:, nodes],
+                    rhs=w_q[h][0][:].bitcast(FP8X4),
+                    rhs_scale=w_q[h][1][:],
+                    start=True,
+                    stop=True,
+                )
+            return g_ps
 
-        a_q = []
+        def group_g(c, h, g_ps, on_scalar):
+            grouped = keep.tile([P, HIDDEN, PACK], BF16, name="g_grp%d%d" % (c, h), align_bytes=64)
+            out, in_ = grouped[:], g_ps[:].rearrange("p t f -> p f t")
+            if on_scalar:
+                nc.scalar.copy(out=out, in_=in_)
+            else:
+                nc.vector.tensor_copy(out=out, in_=in_)
+            return grouped
+
+        def quantise_g(c, h, grouped):
+            cols = slice(h * HIDDEN, (h + 1) * HIDDEN)
+            nc.vector.quantize_mx(
+                out=g_q[c][0][:, cols].bitcast(FP8X4),
+                scales=g_q[c][1][:, cols],
+                in_=grouped[:].rearrange("p f t -> p (f t)"),
+            )
+
         g_q = []
         for c in range(NODE_PASSES):
             g_codes = keep.tile([P, WIDTH], U32, name="g_codes%d" % c, align_bytes=64)
             g_scales = keep.tile([P, WIDTH], U8, name="g_scales%d" % c, align_bytes=64)
-            g_grp = []
-
-            def quantise_g(h):
-                cols = slice(h * HIDDEN, (h + 1) * HIDDEN)
-                nc.vector.quantize_mx(
-                    out=g_codes[:, cols].bitcast(FP8X4),
-                    scales=g_scales[:, cols],
-                    in_=g_grp[h][:].rearrange("p f t -> p (f t)"),
-                )
-
-            for h in range(HEADS):
-                g_ps = banks.tile([P, PACK, HIDDEN], F32, tag="bank", name="g_ps")
-                for t in range(PACK):
-                    x_codes, x_scales = x_q[c][t // 2]
-                    nodes = slice((t % 2) * P, (t % 2 + 1) * P)
-                    nc.tensor.matmul_mx(
-                        out=g_ps[:, t, :],
-                        lhsT=x_codes[:, nodes].bitcast(FP8X4),
-                        lhsT_scale=x_scales[:, nodes],
-                        rhs=w_q[h][0][:].bitcast(FP8X4),
-                        rhs_scale=w_q[h][1][:],
-                        start=True,
-                        stop=True,
-                    )
-                grouped = keep.tile([P, HIDDEN, PACK], BF16, name="g_grp%d%d" % (c, h), align_bytes=64)
-                if h % 2 == 0:
-                    nc.scalar.copy(out=grouped[:], in_=g_ps[:].rearrange("p t f -> p f t"))
-                else:
-                    nc.vector.tensor_copy(out=grouped[:], in_=g_ps[:].rearrange("p t f -> p f t"))
-                g_grp.append(grouped)
-                if h > 0:
-                    quantise_g(h - 1)
-            a_grp = transpose_adj(c)
-            quantise_g(HEADS - 1)
             g_q.append((g_codes, g_scales))
-            a_q.append(quantise_adj(c, a_grp))
-        for i in range(NODE_PASSES, LOOKAHEAD):
-            a_q.append(quantise_adj(i, transpose_adj(i)))
+
+        x_grp0 = [group_x(0, b, transpose_x(0, b)) for b in range(2)]
+        w_grp = [group_w(h) for h in range(HEADS)]
+        x_q = [[quantise_x(0, 0, x_grp0[0])], []]
+        w_q = [quantise_w(0, w_grp[0])]
+        x_q[0].append(quantise_x(0, 1, x_grp0[1]))
+        w_q.extend(quantise_w(h, w_grp[h]) for h in range(1, HEADS))
+        x_grp1 = [group_x(1, b, transpose_x(1, b)) for b in range(2)]
+        g_ps0 = [multiply_g(0, h) for h in range(HEADS)]
+
+        g_grp0 = [group_g(0, 0, g_ps0[0], False), group_g(0, 1, g_ps0[1], True)]
+        x_q[1].extend(quantise_x(1, b, x_grp1[b]) for b in range(2))
+        g_ps1 = [multiply_g(1, h) for h in range(HEADS)]
+        g_grp0.extend((group_g(0, 2, g_ps0[2], False), group_g(0, 3, g_ps0[3], True)))
+        aT = [transpose_adj(i) for i in range(2)]
+        quantise_g(0, 0, g_grp0[0])
+        quantise_g(0, 1, g_grp0[1])
+        g_grp1 = [group_g(1, 0, g_ps1[0], True), group_g(1, 1, g_ps1[1], False)]
+        quantise_g(0, 2, g_grp0[2])
+        quantise_g(0, 3, g_grp0[3])
+        g_grp1.append(group_g(1, 2, g_ps1[2], True))
+        a_grp = [group_adj(0, aT[0])]
+        quantise_g(1, 0, g_grp1[0])
+        g_grp1.append(group_g(1, 3, g_ps1[3], False))
+        a_grp.append(group_adj(1, aT[1]))
+        quantise_g(1, 1, g_grp1[1])
+        quantise_g(1, 2, g_grp1[2])
+        a_q = [quantise_adj(0, a_grp[0])]
+        quantise_g(1, 3, g_grp1[3])
+        for i in range(2, LOOKAHEAD):
+            aT.append(transpose_adj(i))
 
         out_rows = out.rearrange("(p i) d -> p i d", i=ROW_TILES)
-        for i in range(ROW_TILES):
+
+        def multiply_p(i):
             p_ps = banks.tile([P, WIDTH], F32, tag="bank", name="p_ps")
             for c in range(NODE_PASSES):
                 rows = slice(c * P, (c + 1) * P)
@@ -172,13 +202,43 @@ def tile_gat_pa_kernel(tc, x, adj, W0, out):
                     start=(c == 0),
                     stop=(c == NODE_PASSES - 1),
                 )
+            return p_ps
+
+        def exp_p(i, p_ps):
             neg = keep.tile([P, WIDTH], F32, name="neg%d" % i)
             nc.scalar.activation(out=neg[:], in_=p_ps[:], func=ACT.Exp)
-            if i + LOOKAHEAD < ROW_TILES:
-                a_grp = transpose_adj(i + LOOKAHEAD)
-            nc.gpsimd.tensor_scalar(out=neg[:], in0=neg[:], scalar1=1.0, scalar2=0.0, op0=ALU.min, op1=ALU.max)
+            return neg
+
+        def clamp(i, neg):
+            if i < CLAMPS_ON_GPSIMD:
+                nc.gpsimd.tensor_scalar(out=neg[:], in0=neg[:], scalar1=1.0, scalar2=0.0, op0=ALU.min, op1=ALU.max)
+            else:
+                nc.scalar.activation(out=neg[:], in_=neg[:], func=ACT.Relu, scale=-1.0, bias=1.0)
+
+        def finish(i, neg, p_ps):
             res = keep.tile([P, WIDTH], F32, name="res%d" % i)
-            nc.vector.scalar_tensor_tensor(out=res[:], in0=neg[:], scalar=-1.0, in1=p_ps[:], op0=ALU.add, op1=ALU.max)
+            if i < CLAMPS_ON_GPSIMD:
+                nc.vector.scalar_tensor_tensor(
+                    out=res[:], in0=neg[:], scalar=-1.0, in1=p_ps[:], op0=ALU.add, op1=ALU.max
+                )
+            else:
+                nc.vector.scalar_tensor_tensor(
+                    out=res[:], in0=p_ps[:], scalar=0.0, in1=neg[:], op0=ALU.max, op1=ALU.subtract
+                )
             nc.sync.dma_start(out=out_rows[:, i, :], in_=res[:])
+
+        p_ps = []
+        neg = []
+        for i in range(ROW_TILES):
+            p_ps.append(multiply_p(i))
+            neg.append(exp_p(i, p_ps[i]))
+            if i + 2 < ROW_TILES:
+                a_grp.append(group_adj(i + 2, aT[i + 2]))
+            if i + 1 < ROW_TILES:
+                a_q.append(quantise_adj(i + 1, a_grp[i + 1]))
+            clamp(i, neg[i])
+            if i > 0:
+                finish(i - 1, neg[i - 1], p_ps[i - 1])
             if i + LOOKAHEAD < ROW_TILES:
-                a_q.append(quantise_adj(i + LOOKAHEAD, a_grp))
+                aT.append(transpose_adj(i + LOOKAHEAD))
+        finish(ROW_TILES - 1, neg[ROW_TILES - 1], p_ps[ROW_TILES - 1])

@@ -23,7 +23,6 @@ NODE_PASSES = NODES // K_PASS
 ROW_TILES = NODES // P
 ROWS_PER_LOAD = 2
 CLAMPS_ON_GPSIMD = 6
-LOOKAHEAD = 4
 
 FLOPS = 2 * NODES * FEATS * WIDTH + 2 * NODES * NODES * WIDTH
 
@@ -40,23 +39,26 @@ def tile_gat_pa_kernel(tc, x, adj, W0, out):
             nc.vector.quantize_mx(out=codes[:].bitcast(FP8X4), scales=scales[:], in_=grouped)
             return codes, scales
 
+        ctx.enter_context(tc.manual_schedule())
+
         x_sb = []
         w_sb = []
         for c in range(NODE_PASSES):
             x_rows = keep.tile([P, PACK, FEATS], BF16, name="x_sb%d" % c)
-            nc.sync.dma_start(
-                out=x_rows[:].rearrange("p (u e) k -> p u (e k)", u=2),
-                in_=x[c * K_PASS : (c + 1) * K_PASS, :].rearrange("(u p e) k -> p u (e k)", u=2, e=2),
-            )
+            for u in range(2):
+                first = c * K_PASS + u * 2 * P
+                nc.sync.dma_start(
+                    out=x_rows[:, 2 * u : 2 * u + 2, :],
+                    in_=x[first : first + 2 * P, :].rearrange("(p e) k -> p e k", e=2),
+                )
             x_sb.append(x_rows)
-            if c == 0:
-                for h in range(HEADS):
-                    w_rows = keep.tile([P, PACK, HIDDEN], BF16, name="w_sb%d" % h)
-                    nc.sync.dma_start(
-                        out=w_rows[:].rearrange("p (u e) f -> p u (e f)", u=2),
-                        in_=W0[h].rearrange("(u p e) f -> p u (e f)", u=2, e=2),
-                    )
-                    w_sb.append(w_rows)
+            for h in (2 * c, 2 * c + 1):
+                w_rows = keep.tile([P, PACK, HIDDEN], BF16, name="w_sb%d" % h)
+                nc.sync.dma_start(
+                    out=w_rows[:].rearrange("p (u e) f -> p u (e f)", u=2),
+                    in_=W0[h].rearrange("(u p e) f -> p u (e f)", u=2, e=2),
+                )
+                w_sb.append(w_rows)
         adj_rows = adj.rearrange("(p i) m -> p i m", i=ROW_TILES)
         adj_sb = []
         for j in range(ROW_TILES // ROWS_PER_LOAD):
@@ -108,7 +110,7 @@ def tile_gat_pa_kernel(tc, x, adj, W0, out):
         def group_adj(i, aT):
             a_grp = keep.tile([P, NODE_PASSES, P, PACK], BF16, name="a_grp%d" % i, align_bytes=64)
             out, in_ = a_grp[:].bitcast(F32), aT[:].rearrange("p (c u) n -> p c n u", u=2)
-            if i % 3 == 2:
+            if i == ROW_TILES // 2:
                 nc.vector.tensor_copy(out=out, in_=in_)
             else:
                 nc.scalar.copy(out=out, in_=in_)
@@ -156,36 +158,31 @@ def tile_gat_pa_kernel(tc, x, adj, W0, out):
             g_scales = keep.tile([P, WIDTH], U8, name="g_scales%d" % c, align_bytes=64)
             g_q.append((g_codes, g_scales))
 
-        x_grp0 = [group_x(0, b, transpose_x(0, b)) for b in range(2)]
-        w_grp = [group_w(h) for h in range(HEADS)]
-        x_q = [[quantise_x(0, 0, x_grp0[0])], []]
-        w_q = [quantise_w(0, w_grp[0])]
-        x_q[0].append(quantise_x(0, 1, x_grp0[1]))
-        w_q.extend(quantise_w(h, w_grp[h]) for h in range(1, HEADS))
-        x_grp1 = [group_x(1, b, transpose_x(1, b)) for b in range(2)]
-        g_ps0 = [multiply_g(0, h) for h in range(HEADS)]
+        x_grp = [[group_x(0, b, transpose_x(0, b)) for b in range(2)]]
+        w_grp = [group_w(h) for h in range(2)]
+        w_q = [quantise_w(h, w_grp[h]) for h in range(2)]
+        x_q = [[quantise_x(0, b, x_grp[0][b]) for b in range(2)], []]
+        x_grp.append([group_x(1, b, transpose_x(1, b)) for b in range(2)])
+        for b in range(2):
+            w_grp.append(group_w(2 + b))
+            w_q.append(quantise_w(2 + b, w_grp[2 + b]))
+            x_q[1].append(quantise_x(1, b, x_grp[1][b]))
+        g_ps = [[multiply_g(c, h) for h in range(HEADS)] for c in range(NODE_PASSES)]
+        g_grp = [[group_g(c, h, g_ps[c][h], h % 2 == 0) for h in range(HEADS)] for c in range(NODE_PASSES)]
 
-        g_grp0 = [group_g(0, 0, g_ps0[0], False), group_g(0, 1, g_ps0[1], True)]
-        x_q[1].extend(quantise_x(1, b, x_grp1[b]) for b in range(2))
-        g_ps1 = [multiply_g(1, h) for h in range(HEADS)]
-        g_grp0.extend((group_g(0, 2, g_ps0[2], False), group_g(0, 3, g_ps0[3], True)))
-        aT = [transpose_adj(i) for i in range(2)]
-        quantise_g(0, 0, g_grp0[0])
-        quantise_g(0, 1, g_grp0[1])
-        g_grp1 = [group_g(1, 0, g_ps1[0], True), group_g(1, 1, g_ps1[1], False)]
-        quantise_g(0, 2, g_grp0[2])
-        quantise_g(0, 3, g_grp0[3])
-        g_grp1.append(group_g(1, 2, g_ps1[2], True))
+        aT = [transpose_adj(i) for i in range(ROW_TILES)]
+        for h in range(HEADS):
+            quantise_g(0, h, g_grp[0][h])
         a_grp = [group_adj(0, aT[0])]
-        quantise_g(1, 0, g_grp1[0])
-        g_grp1.append(group_g(1, 3, g_ps1[3], False))
-        a_grp.append(group_adj(1, aT[1]))
-        quantise_g(1, 1, g_grp1[1])
-        quantise_g(1, 2, g_grp1[2])
+        for h in range(2):
+            quantise_g(1, h, g_grp[1][h])
         a_q = [quantise_adj(0, a_grp[0])]
-        quantise_g(1, 3, g_grp1[3])
-        for i in range(2, LOOKAHEAD):
-            aT.append(transpose_adj(i))
+        for h in range(2, HEADS):
+            quantise_g(1, h, g_grp[1][h])
+        for i in range(1, ROW_TILES):
+            a_grp.append(group_adj(i, aT[i]))
+        for i in range(1, ROW_TILES):
+            a_q.append(quantise_adj(i, a_grp[i]))
 
         out_rows = out.rearrange("(p i) d -> p i d", i=ROW_TILES)
 
@@ -232,13 +229,7 @@ def tile_gat_pa_kernel(tc, x, adj, W0, out):
         for i in range(ROW_TILES):
             p_ps.append(multiply_p(i))
             neg.append(exp_p(i, p_ps[i]))
-            if i + 2 < ROW_TILES:
-                a_grp.append(group_adj(i + 2, aT[i + 2]))
-            if i + 1 < ROW_TILES:
-                a_q.append(quantise_adj(i + 1, a_grp[i + 1]))
             clamp(i, neg[i])
             if i > 0:
                 finish(i - 1, neg[i - 1], p_ps[i - 1])
-            if i + LOOKAHEAD < ROW_TILES:
-                aT.append(transpose_adj(i + LOOKAHEAD))
         finish(ROW_TILES - 1, neg[ROW_TILES - 1], p_ps[ROW_TILES - 1])

@@ -22,7 +22,8 @@ WIDTH = HEADS * HIDDEN
 NODE_PASSES = NODES // K_PASS
 ROW_TILES = NODES // P
 ROWS_PER_LOAD = 2
-CLAMPS_ON_GPSIMD = 6
+CLAMPS_ON_VECTOR = 2
+CLAMPS_ON_SCALAR = 2
 
 FLOPS = 2 * NODES * FEATS * WIDTH + 2 * NODES * NODES * WIDTH
 
@@ -107,17 +108,23 @@ def tile_gat_pa_kernel(tc, x, adj, W0, out):
                 nc.tensor.transpose(aT[:, s, :], a_words[:, i % ROWS_PER_LOAD, s * P : (s + 1) * P], ident[:])
             return aT
 
+        a_grp = []
+        for j in range(ROW_TILES // 2):
+            a_grp.append(keep.tile([P, 2, NODE_PASSES, P, PACK], BF16, name="a_grp%d" % j, align_bytes=64))
+
         def group_adj(i, aT):
-            a_grp = keep.tile([P, NODE_PASSES, P, PACK], BF16, name="a_grp%d" % i, align_bytes=64)
-            out, in_ = a_grp[:].bitcast(F32), aT[:].rearrange("p (c u) n -> p c n u", u=2)
+            out = a_grp[i // 2][:, i % 2].rearrange("p c n j -> p c (n j)").bitcast(F32).rearrange("p c (n u) -> p c n u", u=2)
+            in_ = aT[:].rearrange("p (c u) n -> p c n u", u=2)
             if i == ROW_TILES // 2:
                 nc.vector.tensor_copy(out=out, in_=in_)
             else:
                 nc.scalar.copy(out=out, in_=in_)
-            return a_grp
 
-        def quantise_adj(i, a_grp):
-            return quantise("a%d" % i, a_grp[:].rearrange("p c n j -> p (c n j)"), NODE_PASSES * P)
+        def quantise_adj(first, count):
+            grouped = a_grp[first // 2][:, first % 2 : first % 2 + count]
+            codes, scales = quantise("a%d" % first, grouped.rearrange("p i c n j -> p (i c n j)"), count * NODE_PASSES * P)
+            width = NODE_PASSES * P
+            return [(codes[:, k * width : (k + 1) * width], scales[:, k * width : (k + 1) * width]) for k in range(count)]
 
         def multiply_g(c, h):
             g_ps = banks.tile([P, PACK, HIDDEN], F32, tag="bank", name="g_ps")
@@ -135,21 +142,24 @@ def tile_gat_pa_kernel(tc, x, adj, W0, out):
                 )
             return g_ps
 
-        def group_g(c, h, g_ps, on_scalar):
-            grouped = keep.tile([P, HIDDEN, PACK], BF16, name="g_grp%d%d" % (c, h), align_bytes=64)
-            out, in_ = grouped[:], g_ps[:].rearrange("p t f -> p f t")
-            if on_scalar:
+        g_grp = []
+        for j in range(NODE_PASSES * HEADS // 2):
+            g_grp.append(keep.tile([P, 2, HIDDEN, PACK], BF16, name="g_grp%d" % j, align_bytes=64))
+
+        def group_g(c, h, g_ps):
+            out = g_grp[(c * HEADS + h) // 2][:, h % 2]
+            in_ = g_ps[:].rearrange("p t f -> p f t")
+            if h % 2 == 0:
                 nc.scalar.copy(out=out, in_=in_)
             else:
                 nc.vector.tensor_copy(out=out, in_=in_)
-            return grouped
 
-        def quantise_g(c, h, grouped):
-            cols = slice(h * HIDDEN, (h + 1) * HIDDEN)
+        def quantise_g(c, h):
+            cols = slice(h * HIDDEN, (h + 2) * HIDDEN)
             nc.vector.quantize_mx(
                 out=g_q[c][0][:, cols].bitcast(FP8X4),
                 scales=g_q[c][1][:, cols],
-                in_=grouped[:].rearrange("p f t -> p (f t)"),
+                in_=g_grp[(c * HEADS + h) // 2][:].rearrange("p h f t -> p (h f t)"),
             )
 
         g_q = []
@@ -163,26 +173,26 @@ def tile_gat_pa_kernel(tc, x, adj, W0, out):
         w_q = [quantise_w(h, w_grp[h]) for h in range(2)]
         x_q = [[quantise_x(0, b, x_grp[0][b]) for b in range(2)], []]
         x_grp.append([group_x(1, b, transpose_x(1, b)) for b in range(2)])
-        for b in range(2):
-            w_grp.append(group_w(2 + b))
-            w_q.append(quantise_w(2 + b, w_grp[2 + b]))
-            x_q[1].append(quantise_x(1, b, x_grp[1][b]))
+        w_grp.extend(group_w(h) for h in range(2, HEADS))
+        w_q.extend(quantise_w(h, w_grp[h]) for h in range(2, HEADS))
+        x_q[1].extend(quantise_x(1, b, x_grp[1][b]) for b in range(2))
         g_ps = [[multiply_g(c, h) for h in range(HEADS)] for c in range(NODE_PASSES)]
-        g_grp = [[group_g(c, h, g_ps[c][h], h % 2 == 0) for h in range(HEADS)] for c in range(NODE_PASSES)]
+        for c in range(NODE_PASSES):
+            for h in range(HEADS):
+                group_g(c, h, g_ps[c][h])
 
         aT = [transpose_adj(i) for i in range(ROW_TILES)]
-        for h in range(HEADS):
-            quantise_g(0, h, g_grp[0][h])
-        a_grp = [group_adj(0, aT[0])]
-        for h in range(2):
-            quantise_g(1, h, g_grp[1][h])
-        a_q = [quantise_adj(0, a_grp[0])]
-        for h in range(2, HEADS):
-            quantise_g(1, h, g_grp[1][h])
+        quantise_g(0, 0)
+        quantise_g(0, 2)
+        group_adj(0, aT[0])
+        quantise_g(1, 0)
+        a_q = quantise_adj(0, 1)
+        quantise_g(1, 2)
         for i in range(1, ROW_TILES):
-            a_grp.append(group_adj(i, aT[i]))
-        for i in range(1, ROW_TILES):
-            a_q.append(quantise_adj(i, a_grp[i]))
+            group_adj(i, aT[i])
+        a_q.extend(quantise_adj(1, 1))
+        for i in range(2, ROW_TILES, 2):
+            a_q.extend(quantise_adj(i, 2))
 
         out_rows = out.rearrange("(p i) d -> p i d", i=ROW_TILES)
 
@@ -207,14 +217,15 @@ def tile_gat_pa_kernel(tc, x, adj, W0, out):
             return neg
 
         def clamp(i, neg):
-            if i < CLAMPS_ON_GPSIMD:
-                nc.gpsimd.tensor_scalar(out=neg[:], in0=neg[:], scalar1=1.0, scalar2=0.0, op0=ALU.min, op1=ALU.max)
+            if i < ROW_TILES - CLAMPS_ON_SCALAR:
+                engine = nc.vector if i < CLAMPS_ON_VECTOR else nc.gpsimd
+                engine.tensor_scalar(out=neg[:], in0=neg[:], scalar1=1.0, scalar2=0.0, op0=ALU.min, op1=ALU.max)
             else:
                 nc.scalar.activation(out=neg[:], in_=neg[:], func=ACT.Relu, scale=-1.0, bias=1.0)
 
         def finish(i, neg, p_ps):
             res = keep.tile([P, WIDTH], F32, name="res%d" % i)
-            if i < CLAMPS_ON_GPSIMD:
+            if i < ROW_TILES - CLAMPS_ON_SCALAR:
                 nc.vector.scalar_tensor_tensor(
                     out=res[:], in0=neg[:], scalar=-1.0, in1=p_ps[:], op0=ALU.add, op1=ALU.max
                 )

@@ -53,13 +53,12 @@ def tile_gat_pa_kernel(tc, x, adj, W0, out):
                     in_=x[first : first + 2 * P, :].rearrange("(p e) k -> p e k", e=2),
                 )
             x_sb.append(x_rows)
-            for h in (2 * c, 2 * c + 1):
-                w_rows = keep.tile([P, PACK, HIDDEN], BF16, name="w_sb%d" % h)
-                nc.sync.dma_start(
-                    out=w_rows[:].rearrange("p (u e) f -> p u (e f)", u=2),
-                    in_=W0[h].rearrange("(u p e) f -> p u (e f)", u=2, e=2),
-                )
-                w_sb.append(w_rows)
+            w_rows = keep.tile([P, 2, PACK, HIDDEN], BF16, name="w_sb%d" % c)
+            nc.sync.dma_start(
+                out=w_rows[:].rearrange("p h t f -> p h (t f)"),
+                in_=W0[2 * c : 2 * c + 2].rearrange("h (p t) f -> p h (t f)", t=PACK),
+            )
+            w_sb.append(w_rows)
         adj_rows = adj.rearrange("(p i) m -> p i m", i=ROW_TILES)
         adj_sb = []
         for j in range(ROW_TILES // ROWS_PER_LOAD):
@@ -79,7 +78,7 @@ def tile_gat_pa_kernel(tc, x, adj, W0, out):
             xT = banks.tile([P, 2, 2, P], F32, tag="bank", name="xT")
             for tl in range(2):
                 for u in range(2):
-                    nc.tensor.transpose(xT[:, tl, u, :], x_words[:, 2 * b + tl, u * P : (u + 1) * P], ident[:])
+                    nc.tensor.transpose(xT[:, tl, u, :], x_words[:, 2 * b + tl, u::2], ident[:])
             return xT
 
         def group_x(c, b, xT):
@@ -94,7 +93,7 @@ def tile_gat_pa_kernel(tc, x, adj, W0, out):
             grouped = keep.tile([P, HIDDEN, PACK], BF16, name="w_grp%d" % h, align_bytes=64)
             nc.vector.tensor_copy(
                 out=grouped[:].rearrange("p (c i) t -> p c t i", i=4),
-                in_=w_sb[h][:].rearrange("p t (c i) -> p c t i", i=4),
+                in_=w_sb[h // 2][:, h % 2].rearrange("p t (c i) -> p c t i", i=4),
             )
             return grouped
 

@@ -73,6 +73,14 @@ def tile_gat_pa_kernel(tc, x, adj, W0, out):
         nc.vector.memset(warm[:], 0.0)
         nc.scalar.activation(out=warm[:], in_=warm[:], func=ACT.Exp)
 
+        zeros = keep.tile([P, WIDTH], BF16, name="zeros")
+        nc.vector.memset(zeros[:], 0.0)
+
+        def keep_clock_up(count):
+            idle = banks.tile([P, WIDTH], F32, tag="bank", name="idle")
+            for n in range(count):
+                nc.tensor.matmul(out=idle[:], lhsT=zeros[:, 0:P], rhs=zeros[:], start=True, stop=True)
+
         def transpose_x(c, b):
             x_words = x_sb[c][:].bitcast(F32)
             xT = banks.tile([P, 2, 2, P], F32, tag="bank", name="xT")
@@ -167,7 +175,9 @@ def tile_gat_pa_kernel(tc, x, adj, W0, out):
             g_scales = keep.tile([P, WIDTH], U8, name="g_scales%d" % c, align_bytes=64)
             g_q.append((g_codes, g_scales))
 
+        keep_clock_up(4)
         x_grp = [[group_x(0, b, transpose_x(0, b)) for b in range(2)]]
+        keep_clock_up(2)
         w_grp = [group_w(h) for h in range(2)]
         w_q = [quantise_w(h, w_grp[h]) for h in range(2)]
         x_q = [[quantise_x(0, b, x_grp[0][b]) for b in range(2)], []]

from contextlib import ExitStack

import concourse.mybir as mybir
from concourse.masks import make_identity

F32 = mybir.dt.float32
BF16 = mybir.dt.bfloat16
U32 = mybir.dt.uint32
U8 = mybir.dt.uint8
FP8X4 = mybir.dt.float8_e4m3fn_x4
ALU = mybir.AluOpType
ACT = mybir.ActivationFunctionType

P = 128
PACK = 4
K_PASS = P * PACK
NODES = 1024
FEATS = 512
HEADS = 4
HIDDEN = 128
WIDTH = HEADS * HIDDEN
NODE_PASSES = NODES // K_PASS
ROW_TILES = NODES // P
ROWS_PER_LOAD = 2
CLAMPS_ON_VECTOR = 2
CLAMPS_ON_SCALAR = 2

FLOPS = 2 * NODES * FEATS * WIDTH + 2 * NODES * NODES * WIDTH


def tile_gat_pa_kernel(tc, x, adj, W0, out):
    nc = tc.nc
    with ExitStack() as ctx:
        keep = ctx.enter_context(tc.tile_pool(name="keep", bufs=1))
        banks = ctx.enter_context(tc.psum_pool(name="banks", bufs=8))

        def quantise(name, grouped, width):
            codes = keep.tile([P, width], U32, name=name + "_codes", align_bytes=64)
            scales = keep.tile([P, width], U8, name=name + "_scales", align_bytes=64)
            nc.vector.quantize_mx(out=codes[:].bitcast(FP8X4), scales=scales[:], in_=grouped)
            return codes, scales

        ctx.enter_context(tc.manual_schedule())

        x_sb = []
        w_sb = []
        for c in range(NODE_PASSES):
            x_rows = keep.tile([P, PACK, FEATS], BF16, name="x_sb%d" % c)
            for u in range(2):
                first = c * K_PASS + u * 2 * P
                nc.sync.dma_start(
                    out=x_rows[:, 2 * u : 2 * u + 2, :],
                    in_=x[first : first + 2 * P, :].rearrange("(p e) k -> p e k", e=2),
                )
            x_sb.append(x_rows)
            w_rows = keep.tile([P, 2, PACK, HIDDEN], BF16, name="w_sb%d" % c)
            nc.sync.dma_start(
                out=w_rows[:].rearrange("p h t f -> p h (t f)"),
                in_=W0[2 * c : 2 * c + 2].rearrange("h (p t) f -> p h (t f)", t=PACK),
            )
            w_sb.append(w_rows)
        adj_rows = adj.rearrange("(p i) m -> p i m", i=ROW_TILES)
        adj_sb = []
        for j in range(ROW_TILES // ROWS_PER_LOAD):
            a_rows = keep.tile([P, ROWS_PER_LOAD, NODES], BF16, name="adj_sb%d" % j)
            nc.sync.dma_start(out=a_rows[:], in_=adj_rows[:, j * ROWS_PER_LOAD : (j + 1) * ROWS_PER_LOAD, :])
            adj_sb.append(a_rows)

        ident = keep.tile([P, P], F32, name="ident")
        make_identity(nc, ident[:])

        warm = keep.tile([P, 1], F32, name="warm")
        nc.vector.memset(warm[:], 0.0)
        nc.scalar.activation(out=warm[:], in_=warm[:], func=ACT.Exp)

        zeros = keep.tile([P, WIDTH], BF16, name="zeros")
        nc.vector.memset(zeros[:], 0.0)

        def keep_clock_up(count):
            idle = banks.tile([P, WIDTH], F32, tag="bank", name="idle")
            for n in range(count):
                nc.tensor.matmul(out=idle[:], lhsT=zeros[:, 0:P], rhs=zeros[:], start=True, stop=True)

        def transpose_x(c, b):
            x_words = x_sb[c][:].bitcast(F32)
            xT = banks.tile([P, 2, 2, P], F32, tag="bank", name="xT")
            for tl in range(2):
                for u in range(2):
                    nc.tensor.transpose(xT[:, tl, u, :], x_words[:, 2 * b + tl, u::2], ident[:])
            return xT

        def group_x(c, b, xT):
            x_grp = keep.tile([P, 2, P, PACK], BF16, name="x_grp%d%d" % (c, b), align_bytes=64)
            nc.scalar.copy(out=x_grp[:].bitcast(F32), in_=xT[:].rearrange("p t u n -> p t n u"))
            return x_grp

        def quantise_x(c, b, x_grp):
            return quantise("x%d%d" % (c, b), x_grp[:].rearrange("p t n j -> p (t n j)"), 2 * P)

        def group_w(h):
            grouped = keep.tile([P, HIDDEN, PACK], BF16, name="w_grp%d" % h, align_bytes=64)
            nc.vector.tensor_copy(
                out=grouped[:].rearrange("p (c i) t -> p c t i", i=4),
                in_=w_sb[h // 2][:, h % 2].rearrange("p t (c i) -> p c t i", i=4),
            )
            return grouped

        def quantise_w(h, grouped):
            return quantise("w%d" % h, grouped[:].rearrange("p f t -> p (f t)"), HIDDEN)

        def transpose_adj(i):
            a_words = adj_sb[i // ROWS_PER_LOAD][:].bitcast(F32)
            aT = banks.tile([P, PACK, P], F32, tag="bank", name="aT")
            for s in range(PACK):
                nc.tensor.transpose(aT[:, s, :], a_words[:, i % ROWS_PER_LOAD, s * P : (s + 1) * P], ident[:])
            return aT

        a_grp = []
        for j in range(ROW_TILES // 2):
            a_grp.append(keep.tile([P, 2, NODE_PASSES, P, PACK], BF16, name="a_grp%d" % j, align_bytes=64))

        def group_adj(i, aT):
            out = a_grp[i // 2][:, i % 2].rearrange("p c n j -> p c (n j)").bitcast(F32).rearrange("p c (n u) -> p c n u", u=2)
            in_ = aT[:].rearrange("p (c u) n -> p c n u", u=2)
            if i == ROW_TILES // 2:
                nc.vector.tensor_copy(out=out, in_=in_)
            else:
                nc.scalar.copy(out=out, in_=in_)

        def quantise_adj(first, count):
            grouped = a_grp[first // 2][:, first % 2 : first % 2 + count]
            codes, scales = quantise("a%d" % first, grouped.rearrange("p i c n j -> p (i c n j)"), count * NODE_PASSES * P)
            width = NODE_PASSES * P
            return [(codes[:, k * width : (k + 1) * width], scales[:, k * width : (k + 1) * width]) for k in range(count)]

        def multiply_g(c, h):
            g_ps = banks.tile([P, PACK, HIDDEN], F32, tag="bank", name="g_ps")
            for t in range(PACK):
                x_codes, x_scales = x_q[c][t // 2]
                nodes = slice((t % 2) * P, (t % 2 + 1) * P)
                nc.tensor.matmul_mx(
                    out=g_ps[:, t, :],
                    lhsT=x_codes[:, nodes].bitcast(FP8X4),
                    lhsT_scale=x_scales[:, nodes],
                    rhs=w_q[h][0][:].bitcast(FP8X4),
                    rhs_scale=w_q[h][1][:],
                    start=True,
                    stop=True,
                )
            return g_ps

        g_grp = []
        for j in range(NODE_PASSES * HEADS // 2):
            g_grp.append(keep.tile([P, 2, HIDDEN, PACK], BF16, name="g_grp%d" % j, align_bytes=64))

        def group_g(c, h, g_ps):
            out = g_grp[(c * HEADS + h) // 2][:, h % 2]
            in_ = g_ps[:].rearrange("p t f -> p f t")
            if h % 2 == 0:
                nc.scalar.copy(out=out, in_=in_)
            else:
                nc.vector.tensor_copy(out=out, in_=in_)

        def quantise_g(c, h):
            cols = slice(h * HIDDEN, (h + 2) * HIDDEN)
            nc.vector.quantize_mx(
                out=g_q[c][0][:, cols].bitcast(FP8X4),
                scales=g_q[c][1][:, cols],
                in_=g_grp[(c * HEADS + h) // 2][:].rearrange("p h f t -> p (h f t)"),
            )

        g_q = []
        for c in range(NODE_PASSES):
            g_codes = keep.tile([P, WIDTH], U32, name="g_codes%d" % c, align_bytes=64)
            g_scales = keep.tile([P, WIDTH], U8, name="g_scales%d" % c, align_bytes=64)
            g_q.append((g_codes, g_scales))

        keep_clock_up(4)
        x_grp = [[group_x(0, b, transpose_x(0, b)) for b in range(2)]]
        keep_clock_up(2)
        w_grp = [group_w(h) for h in range(2)]
        w_q = [quantise_w(h, w_grp[h]) for h in range(2)]
        x_q = [[quantise_x(0, b, x_grp[0][b]) for b in range(2)], []]
        x_grp.append([group_x(1, b, transpose_x(1, b)) for b in range(2)])
        w_grp.extend(group_w(h) for h in range(2, HEADS))
        w_q.extend(quantise_w(h, w_grp[h]) for h in range(2, HEADS))
        x_q[1].extend(quantise_x(1, b, x_grp[1][b]) for b in range(2))
        g_ps = [[multiply_g(c, h) for h in range(HEADS)] for c in range(NODE_PASSES)]
        for c in range(NODE_PASSES):
            for h in range(HEADS):
                group_g(c, h, g_ps[c][h])

        aT = [transpose_adj(i) for i in range(ROW_TILES)]
        quantise_g(0, 0)
        quantise_g(0, 2)
        group_adj(0, aT[0])
        quantise_g(1, 0)
        a_q = quantise_adj(0, 1)
        quantise_g(1, 2)
        for i in range(1, ROW_TILES):
            group_adj(i, aT[i])
        a_q.extend(quantise_adj(1, 1))
        for i in range(2, ROW_TILES, 2):
            a_q.extend(quantise_adj(i, 2))

        out_rows = out.rearrange("(p i) d -> p i d", i=ROW_TILES)

        def multiply_p(i):
            p_ps = banks.tile([P, WIDTH], F32, tag="bank", name="p_ps")
            for c in range(NODE_PASSES):
                rows = slice(c * P, (c + 1) * P)
                nc.tensor.matmul_mx(
                    out=p_ps[:],
                    lhsT=a_q[i][0][:, rows].bitcast(FP8X4),
                    lhsT_scale=a_q[i][1][:, rows],
                    rhs=g_q[c][0][:].bitcast(FP8X4),
                    rhs_scale=g_q[c][1][:],
                    start=(c == 0),
                    stop=(c == NODE_PASSES - 1),
                )
            return p_ps

        def exp_p(i, p_ps):
            neg = keep.tile([P, WIDTH], F32, name="neg%d" % i)
            nc.scalar.activation(out=neg[:], in_=p_ps[:], func=ACT.Exp)
            return neg

        def clamp(i, neg):
            if i < ROW_TILES - CLAMPS_ON_SCALAR:
                engine = nc.vector if i < CLAMPS_ON_VECTOR else nc.gpsimd
                engine.tensor_scalar(out=neg[:], in0=neg[:], scalar1=1.0, scalar2=0.0, op0=ALU.min, op1=ALU.max)
            else:
                nc.scalar.activation(out=neg[:], in_=neg[:], func=ACT.Relu, scale=-1.0, bias=1.0)

        def finish(i, neg, p_ps):
            res = keep.tile([P, WIDTH], F32, name="res%d" % i)
            if i < ROW_TILES - CLAMPS_ON_SCALAR:
                nc.vector.scalar_tensor_tensor(
                    out=res[:], in0=neg[:], scalar=-1.0, in1=p_ps[:], op0=ALU.add, op1=ALU.max
                )
            else:
                nc.vector.scalar_tensor_tensor(
                    out=res[:], in0=p_ps[:], scalar=0.0, in1=neg[:], op0=ALU.max, op1=ALU.subtract
                )
            nc.sync.dma_start(out=out_rows[:, i, :], in_=res[:])

        p_ps = []
        neg = []
        for i in range(ROW_TILES):
            p_ps.append(multiply_p(i))
            neg.append(exp_p(i, p_ps[i]))
            clamp(i, neg[i])
            if i > 0:
                finish(i - 1, neg[i - 1], p_ps[i - 1])
        finish(ROW_TILES - 1, neg[ROW_TILES - 1], p_ps[ROW_TILES - 1])
